import numpy as np
import ml_dtypes


def mxq(x, axis, fmt="e4m3"):
    dtype, down = {"e4m3": (ml_dtypes.float8_e4m3fn, 7), "e5m2": (ml_dtypes.float8_e5m2, 14)}[fmt]
    v = np.moveaxis(np.asarray(x, np.float32).astype(ml_dtypes.bfloat16).astype(np.float64), axis, -1)
    blocks = v.reshape(v.shape[:-1] + (-1, 32))
    amax = np.abs(blocks).max(-1, keepdims=True)
    byte = np.maximum(np.where(amax > 0, np.frexp(amax)[1] - 1 + 127, 0) - down, 1)
    scale = np.exp2(byte - 127.0)
    codes = (blocks / scale).astype(np.float32).astype(dtype).astype(np.float64)
    return np.moveaxis((codes * scale).reshape(v.shape), -1, axis)


WIDE = False


def mx_kscale(k):
    if not WIDE:
        return np.ones(k)
    levels = np.array([10, -10, 5, -5, 0])
    a = np.random.permutation(np.resize(levels, k // 512 * 4)).reshape(k // 512, 4)
    idx = np.arange(k)
    return np.exp2(a[idx // 512, idx % 128 // 32])


BF16 = ml_dtypes.bfloat16


def bf(x):
    return np.asarray(x, np.float32).astype(BF16)


def f64(x):
    return np.asarray(x).astype(np.float64)


E2M1 = np.array([0.0, 0.5, 1.0, 1.5, 2.0, 3.0, 4.0, 6.0, -0.0, -0.5, -1.0, -1.5, -2.0, -3.0, -4.0, -6.0])


def pack_weight(w, fmt):
    k, n = w.shape
    w = f64(bf(w)).reshape(k // 32, 32, n)
    amax = np.abs(w).max(1)
    if fmt == "e4m3":
        byte = np.frexp(amax)[1] - 1 + 127 - 7
    else:
        mant, ex = np.frexp(amax / 6.0)
        byte = np.where(mant > 0.5, ex, ex - 1) + 127
    byte = np.clip(np.where(amax > 0, byte, 1), 1, 254)
    scaled = (w * np.exp2(127.0 - byte)[:, None, :]).reshape(k, n).astype(np.float32)
    by_word = np.ascontiguousarray(scaled.reshape(k // 512, 128, 4, n).transpose(0, 1, 3, 2))
    if fmt == "e4m3":
        words = by_word.astype(ml_dtypes.float8_e4m3fn).view(np.uint8)
    else:
        c = by_word.astype(ml_dtypes.float4_e2m1fn).view(np.uint8) & 0xF
        words = c[..., 0::2] | (c[..., 1::2] << 4)
    return np.ascontiguousarray(words), np.ascontiguousarray(byte.astype(np.uint8).reshape(k // 512, 16, n))


def unpack_weight(words, scales, fmt):
    g, p, n, _ = words.shape
    if fmt == "e4m3":
        vals = np.ascontiguousarray(words).view(ml_dtypes.float8_e4m3fn).astype(np.float64)
    else:
        nib = np.empty((g, p, n, 4), np.uint8)
        nib[..., 0::2] = words & 0xF
        nib[..., 1::2] = words >> 4
        vals = E2M1[nib]
    vals = vals * np.repeat(np.exp2(scales.astype(np.float64) - 127.0), 8, axis=1)[..., None]
    return vals.transpose(0, 1, 3, 2).reshape(g * 512, n)


B, I, H = 128, 1024, 2048
FMT = "e4m3"


def sigmoid(v):
    return 1.0 / (1.0 + np.exp(-v))


def setup_inputs():
    s = mx_kscale(I + H)
    sx, sh = s[:I], s[I:]

    def wx():
        return pack_weight((np.random.standard_normal((H, I)) * 0.7 / np.sqrt(I) / sx).T, FMT)

    def wh():
        return pack_weight((np.random.standard_normal((H, H)) * 0.7 / np.sqrt(H) / sh).T, FMT)

    def bias():
        return bf(np.random.standard_normal(H) * 0.3)

    out = {}
    out["x"] = bf(np.random.standard_normal((B, I)) * sx)
    out["h"] = bf(np.random.standard_normal((B, H)) * sh)
    out["c"] = bf(np.random.standard_normal((B, H)))
    for name in ("weight_ii", "weight_if", "weight_ig", "weight_io"):
        words, scales = wx()
        out[name + "_words"] = words
        out[name + "_scales"] = scales
    for name in ("weight_hi", "weight_hf", "weight_hg", "weight_ho"):
        words, scales = wh()
        out[name + "_words"] = words
        out[name + "_scales"] = scales
    for name in ("bias_i", "bias_f", "bias_g", "bias_o"):
        out[name] = bias()
    return out


def reference(x, h, c,
              weight_ii_words, weight_ii_scales, weight_if_words, weight_if_scales,
              weight_ig_words, weight_ig_scales, weight_io_words, weight_io_scales,
              weight_hi_words, weight_hi_scales, weight_hf_words, weight_hf_scales,
              weight_hg_words, weight_hg_scales, weight_ho_words, weight_ho_scales,
              bias_i, bias_f, bias_g, bias_o):
    W_x = np.concatenate([unpack_weight(weight_ii_words, weight_ii_scales, FMT).T,
                          unpack_weight(weight_if_words, weight_if_scales, FMT).T,
                          unpack_weight(weight_ig_words, weight_ig_scales, FMT).T,
                          unpack_weight(weight_io_words, weight_io_scales, FMT).T], axis=0)
    W_h = np.concatenate([unpack_weight(weight_hi_words, weight_hi_scales, FMT).T,
                          unpack_weight(weight_hf_words, weight_hf_scales, FMT).T,
                          unpack_weight(weight_hg_words, weight_hg_scales, FMT).T,
                          unpack_weight(weight_ho_words, weight_ho_scales, FMT).T], axis=0)
    b = np.concatenate([f64(bias_i), f64(bias_f), f64(bias_g), f64(bias_o)], axis=0)
    z = np.concatenate([f64(x), f64(h)], axis=1)
    W = np.concatenate([W_x, W_h], axis=1)
    gates = (mxq(z, 1, "e4m3") @ W.T) + b
    gi, gf, gg, go = np.split(gates, 4, axis=1)
    i = sigmoid(gi)
    f = sigmoid(gf)
    g = np.tanh(gg)
    o = sigmoid(go)
    c_new = f * c_in(c) + i * g
    h_new = o * np.tanh(c_new)
    return (h_new, c_new)


def c_in(c):
    return f64(c)

@@ -1,0 +1,243 @@
+from contextlib import ExitStack
+
+import concourse.mybir as mybir
+from concourse.masks import make_identity
+
+F32 = mybir.dt.float32
+BF16 = mybir.dt.bfloat16
+I32 = mybir.dt.int32
+U32 = mybir.dt.uint32
+U8 = mybir.dt.uint8
+FP8X4 = mybir.dt.float8_e4m3fn_x4
+ACT = mybir.ActivationFunctionType
+
+P = 128
+PACK = 4
+K_PASS = P * PACK
+X_PASSES = 2
+H_PASSES = 4
+PASSES = X_PASSES + H_PASSES
+HIDDEN = 2048
+CHUNK = 512
+CHUNKS = HIDDEN // CHUNK
+GATES = 4
+QUADRANTS = 4
+PLANES_PER_SLOT = 4
+PLANE_SLOTS = GATES * PASSES // PLANES_PER_SLOT
+WEIGHT_BUFS = 12
+COMBINE_LAG = 2
+
+FLOPS = 2 * P * (PASSES * K_PASS) * (GATES * HIDDEN)
+
+
+def tile_forcedgpulstmcell_w_kernel(
+    tc,
+    x,
+    h,
+    c,
+    weight_ii_words,
+    weight_ii_scales,
+    weight_if_words,
+    weight_if_scales,
+    weight_ig_words,
+    weight_ig_scales,
+    weight_io_words,
+    weight_io_scales,
+    weight_hi_words,
+    weight_hi_scales,
+    weight_hf_words,
+    weight_hf_scales,
+    weight_hg_words,
+    weight_hg_scales,
+    weight_ho_words,
+    weight_ho_scales,
+    bias_i,
+    bias_f,
+    bias_g,
+    bias_o,
+    h_new,
+    c_new,
+):
+    nc = tc.nc
+
+    INPUT, CANDIDATE, FORGET, OUTPUT = range(GATES)
+    x_words = (weight_ii_words, weight_ig_words, weight_if_words, weight_io_words)
+    x_scales = (weight_ii_scales, weight_ig_scales, weight_if_scales, weight_io_scales)
+    h_words = (weight_hi_words, weight_hg_words, weight_hf_words, weight_ho_words)
+    h_scales = (weight_hi_scales, weight_hg_scales, weight_hf_scales, weight_ho_scales)
+    biases = (bias_i, bias_g, bias_f, bias_o)
+    functions = (ACT.Sigmoid, ACT.Tanh, ACT.Sigmoid, ACT.Sigmoid)
+
+    with ExitStack() as ctx:
+        ctx.enter_context(tc.manual_schedule())
+        keep = ctx.enter_context(tc.tile_pool(name="keep", bufs=1))
+        weights = ctx.enter_context(tc.tile_pool(name="weights", bufs=WEIGHT_BUFS))
+        gate_pool = ctx.enter_context(tc.tile_pool(name="gate", bufs=2))
+        work = ctx.enter_context(tc.tile_pool(name="work", bufs=3))
+        acc_psum = ctx.enter_context(tc.psum_pool(name="acc", bufs=6))
+        aux_psum = ctx.enter_context(tc.psum_pool(name="aux", bufs=2))
+
+        bias_rows = keep.tile([P, CHUNK], BF16)
+        nc.vector.memset(bias_rows[:], 0.0)
+        planes = keep.tile([P, PLANE_SLOTS, HIDDEN], U8, align_bytes=64)
+        nc.vector.memset(planes[:].rearrange("p s n -> p (s n)").bitcast(I32), 0)
+
+        ident_f32 = keep.tile([P, P], F32)
+        make_identity(nc, ident_f32[:])
+        ident_bf16 = keep.tile([P, P], BF16)
+        make_identity(nc, ident_bf16[:])
+
+        z_sb = keep.tile([P, PASSES * K_PASS], BF16)
+        nc.sync.dma_start(out=z_sb[:, 0 : X_PASSES * K_PASS], in_=x)
+        nc.sync.dma_start(out=z_sb[:, X_PASSES * K_PASS :], in_=h)
+
+        for a in range(GATES):
+            nc.scalar.dma_start(
+                out=bias_rows[CHUNKS * a : CHUNKS * (a + 1), :],
+                in_=biases[a].rearrange("(j n) -> j n", j=CHUNKS),
+            )
+
+        def plane_of(a, g):
+            if g >= X_PASSES:
+                return a, PACK * (g - X_PASSES)
+            return GATES + a // 2, PACK * (X_PASSES * (a % 2) + g)
+
+        def load_scales(a):
+            x_slot, x_offset = plane_of(a, 0)
+            h_slot, h_offset = plane_of(a, X_PASSES)
+            for quadrant in range(QUADRANTS):
+                rows = slice(PACK * quadrant, PACK * (quadrant + 1))
+                first = 32 * quadrant
+                nc.gpsimd.dma_start(
+                    out=planes[first + x_offset : first + x_offset + PACK * X_PASSES, x_slot, :].bitcast(F32),
+                    in_=x_scales[a][:, rows, :].bitcast(F32),
+                )
+                nc.gpsimd.dma_start(
+                    out=planes[first + h_offset : first + h_offset + PACK * H_PASSES, h_slot, :].bitcast(F32),
+                    in_=h_scales[a][:, rows, :].bitcast(F32),
+                )
+
+        for a in range(GATES):
+            load_scales(a)
+
+        n_tiles = GATES * PASSES
+        weight_tiles = {}
+
+        def load_weights(i):
+            a, g = divmod(i, PASSES)
+            source = x_words[a][g] if g < X_PASSES else h_words[a][g - X_PASSES]
+            source = source.rearrange("p n t -> p (n t)")
+            w = weights.tile([P, HIDDEN], U32, tag="w", align_bytes=64)
+            weight_tiles[i] = w
+            pieces = CHUNKS if i == n_tiles - 1 else 1
+            width = HIDDEN // pieces
+            for piece in range(pieces):
+                nc.sync.dma_start(
+                    out=w[:, piece * width : (piece + 1) * width].bitcast(I32),
+                    in_=source[:, PACK * piece * width : PACK * (piece + 1) * width].bitcast(I32),
+                )
+
+        for i in range(WEIGHT_BUFS):
+            load_weights(i)
+
+        c_sb = keep.tile([P, HIDDEN], BF16)
+        nc.sync.dma_start(out=c_sb[:], in_=c)
+
+        z_words = z_sb[:].bitcast(F32)
+        grouped = keep.tile([P, PASSES, P, PACK], BF16, align_bytes=64)
+        grouped_words = grouped[:].bitcast(F32)
+        for pair in range(PASSES // 2):
+            flipped = aux_psum.tile([P, 2, 2, P], F32, tag="aux")
+            for half in range(2):
+                g = 2 * pair + half
+                for u in range(2):
+                    nc.tensor.transpose(
+                        flipped[:, half, u, :],
+                        z_words[:, 256 * g + u : 256 * (g + 1) : 2],
+                        ident_f32[:],
+                    )
+            copy = nc.vector.tensor_copy if pair % 2 == 0 else nc.scalar.copy
+            copy(
+                out=grouped_words[:, 2 * pair : 2 * pair + 2, :, :],
+                in_=flipped[:].rearrange("p g u b -> p g b u"),
+            )
+
+        z_codes = keep.tile([P, PASSES, P], U32, align_bytes=64)
+        z_scales = keep.tile([P, PASSES, P], U8, align_bytes=64)
+        for first, count in ((0, X_PASSES), (X_PASSES, H_PASSES)):
+            passes = slice(first, first + count)
+            nc.vector.quantize_mx(
+                out=z_codes[:, passes, :].rearrange("p g b -> p (g b)").bitcast(FP8X4),
+                scales=z_scales[:, passes, :].rearrange("p g b -> p (g b)"),
+                in_=grouped[:, passes, :, :].rearrange("p g b t -> p (g b t)"),
+            )
+
+        bias_all = keep.tile([P, GATES, HIDDEN], F32)
+        for a in range(GATES):
+            for j in range(CHUNKS):
+                row = CHUNKS * a + j
+                spread = aux_psum.tile([P, CHUNK], F32, tag="aux")
+                nc.tensor.matmul(
+                    spread[:],
+                    lhsT=ident_bf16[:, row : row + 1].to_broadcast([P, P]),
+                    rhs=bias_rows[:],
+                    start=True,
+                    stop=True,
+                )
+                copy = nc.vector.tensor_copy if j % 2 == 0 else nc.scalar.copy
+                copy(out=bias_all[:, a, j * CHUNK : (j + 1) * CHUNK], in_=spread[:])
+
+        update = keep.tile([P, HIDDEN], F32)
+        c_next = keep.tile([P, HIDDEN], F32)
+        tanh_c = keep.tile([P, HIDDEN], F32)
+        h_next = keep.tile([P, HIDDEN], F32)
+        activated = {}
+
+        def activate(a, acc, j):
+            cols = slice(j * CHUNK, (j + 1) * CHUNK)
+            pre = work.tile([P, CHUNK], F32, tag="pre")
+            nc.vector.tensor_add(out=pre[:], in0=acc[j][:], in1=bias_all[:, a, cols])
+            nc.scalar.activation(out=activated[a][:, cols], in_=pre[:], func=functions[a])
+
+        def combine(a, j):
+            cols = slice(j * CHUNK, (j + 1) * CHUNK)
+            if a == CANDIDATE:
+                nc.vector.tensor_mul(out=update[:, cols], in0=activated[INPUT][:, cols], in1=activated[a][:, cols])
+            if a == FORGET:
+                kept = work.tile([P, CHUNK], F32, tag="kept")
+                nc.vector.tensor_mul(out=kept[:], in0=activated[a][:, cols], in1=c_sb[:, cols])
+                nc.vector.tensor_add(out=c_next[:, cols], in0=kept[:], in1=update[:, cols])
+                nc.scalar.activation(out=tanh_c[:, cols], in_=c_next[:, cols], func=ACT.Tanh)
+            if a == OUTPUT:
+                nc.vector.tensor_mul(out=h_next[:, cols], in0=activated[a][:, cols], in1=tanh_c[:, cols])
+                nc.sync.dma_start(out=h_new[:, cols], in_=h_next[:, cols])
+
+        acc = []
+        for i in range(n_tiles):
+            a, g = divmod(i, PASSES)
+            if g == 0:
+                acc = [acc_psum.tile([P, CHUNK], F32, name="acc%d" % j, tag="acc") for j in range(CHUNKS)]
+            slot, offset = plane_of(a, g)
+            w = weight_tiles[i]
+            for j in range(CHUNKS):
+                cols = slice(j * CHUNK, (j + 1) * CHUNK)
+                nc.tensor.matmul_mx(
+                    out=acc[j][:],
+                    lhsT=z_codes[:, g, :].bitcast(FP8X4),
+                    lhsT_scale=z_scales[:, g, :],
+                    rhs=w[:, cols].bitcast(FP8X4),
+                    rhs_scale=planes[offset:P, slot, cols],
+                    start=(g == 0),
+                    stop=(g == PASSES - 1),
+                )
+            if i + WEIGHT_BUFS < n_tiles:
+                load_weights(i + WEIGHT_BUFS)
+            if g == PASSES - 1:
+                activated[a] = gate_pool.tile([P, HIDDEN], F32, name="activated%d" % a, tag="activated")
+                for j in range(CHUNKS + COMBINE_LAG):
+                    if j < CHUNKS:
+                        activate(a, acc, j)
+                    if j >= COMBINE_LAG:
+                        combine(a, j - COMBINE_LAG)
+                if a == FORGET:
+                    nc.sync.dma_start(out=c_new, in_=c_next[:])

@@ -26,6 +26,12 @@ PLANES_PER_SLOT = 4
 PLANE_SLOTS = GATES * PASSES // PLANES_PER_SLOT
 WEIGHT_BUFS = 12
 COMBINE_LAG = 2
+LAST_WIDTH = 256
+OUTPUT_GROUPS = (
+    (0, 1024, ((0, 2), (2, 2), (4, 2))),
+    (1024, 512, ((0, 2), (2, 4))),
+    (1536, 512, ((0, 2), (2, 2), (4, 1), (5, 1))),
+)
 
 FLOPS = 2 * P * (PASSES * K_PASS) * (GATES * HIDDEN)
 
@@ -120,22 +126,19 @@ def tile_forcedgpulstmcell_w_kernel(
         for a in range(GATES):
             load_scales(a)
 
-        n_tiles = GATES * PASSES
+        loads = [(a, g, 1, 0, HIDDEN) for a in (INPUT, CANDIDATE, FORGET) for g in range(PASSES)]
+        for first_col, columns, parts in OUTPUT_GROUPS:
+            for first_pass, count in parts:
+                loads.append((OUTPUT, first_pass, count, first_col, columns))
         weight_tiles = {}
 
         def load_weights(i):
-            a, g = divmod(i, PASSES)
-            source = x_words[a][g] if g < X_PASSES else h_words[a][g - X_PASSES]
-            source = source.rearrange("p n t -> p (n t)")
-            w = weights.tile([P, HIDDEN], U32, tag="w", align_bytes=64)
+            a, g, count, first_col, columns = loads[i]
+            source = x_words[a][g : g + count] if g < X_PASSES else h_words[a][g - X_PASSES : g - X_PASSES + count]
+            source = source.rearrange("g p n t -> g p (n t)")[:, :, PACK * first_col : PACK * (first_col + columns)]
+            w = weights.tile([P, count, columns], U32, tag="w", align_bytes=64)
             weight_tiles[i] = w
-            pieces = CHUNKS if i == n_tiles - 1 else 1
-            width = HIDDEN // pieces
-            for piece in range(pieces):
-                nc.sync.dma_start(
-                    out=w[:, piece * width : (piece + 1) * width].bitcast(I32),
-                    in_=source[:, PACK * piece * width : PACK * (piece + 1) * width].bitcast(I32),
-                )
+            nc.sync.dma_start(out=w[:].bitcast(I32), in_=source.rearrange("g p b -> p g b").bitcast(I32))
 
         for i in range(WEIGHT_BUFS):
             load_weights(i)
@@ -193,14 +196,13 @@ def tile_forcedgpulstmcell_w_kernel(
         h_next = keep.tile([P, HIDDEN], F32)
         activated = {}
 
-        def activate(a, acc, j):
-            cols = slice(j * CHUNK, (j + 1) * CHUNK)
+        def activate(a, bank, local, cols):
             pre = work.tile([P, CHUNK], F32, tag="pre")
-            nc.vector.tensor_add(out=pre[:], in0=acc[j][:], in1=bias_all[:, a, cols])
-            nc.scalar.activation(out=activated[a][:, cols], in_=pre[:], func=functions[a])
+            width = cols.stop - cols.start
+            nc.vector.tensor_add(out=pre[:, 0:width], in0=bank[:, local], in1=bias_all[:, a, cols])
+            nc.scalar.activation(out=activated[a][:, cols], in_=pre[:, 0:width], func=functions[a])
 
-        def combine(a, j):
-            cols = slice(j * CHUNK, (j + 1) * CHUNK)
+        def combine(a, cols):
             if a == CANDIDATE:
                 nc.vector.tensor_mul(out=update[:, cols], in0=activated[INPUT][:, cols], in1=activated[a][:, cols])
             if a == FORGET:
@@ -212,32 +214,41 @@ def tile_forcedgpulstmcell_w_kernel(
                 nc.vector.tensor_mul(out=h_next[:, cols], in0=activated[a][:, cols], in1=tanh_c[:, cols])
                 nc.sync.dma_start(out=h_new[:, cols], in_=h_next[:, cols])
 
-        acc = []
-        for i in range(n_tiles):
-            a, g = divmod(i, PASSES)
+        banks = {}
+        for i, (a, g, count, first_col, columns) in enumerate(loads):
+            chunks = range(first_col // CHUNK, (first_col + columns) // CHUNK)
             if g == 0:
-                acc = [acc_psum.tile([P, CHUNK], F32, name="acc%d" % j, tag="acc") for j in range(CHUNKS)]
-            slot, offset = plane_of(a, g)
+                if first_col == 0:
+                    activated[a] = gate_pool.tile([P, HIDDEN], F32, name="activated%d" % a, tag="activated")
+                for j in chunks:
+                    banks[j] = acc_psum.tile([P, CHUNK], F32, name="acc%d" % j, tag="acc")
             w = weight_tiles[i]
-            for j in range(CHUNKS):
-                cols = slice(j * CHUNK, (j + 1) * CHUNK)
-                nc.tensor.matmul_mx(
-                    out=acc[j][:],
-                    lhsT=z_codes[:, g, :].bitcast(FP8X4),
-                    lhsT_scale=z_scales[:, g, :],
-                    rhs=w[:, cols].bitcast(FP8X4),
-                    rhs_scale=planes[offset:P, slot, cols],
-                    start=(g == 0),
-                    stop=(g == PASSES - 1),
-                )
-            if i + WEIGHT_BUFS < n_tiles:
+            for step in range(count):
+                slot, offset = plane_of(a, g + step)
+                for j in chunks:
+                    cols = slice(j * CHUNK, (j + 1) * CHUNK)
+                    nc.tensor.matmul_mx(
+                        out=banks[j][:],
+                        lhsT=z_codes[:, g + step, :].bitcast(FP8X4),
+                        lhsT_scale=z_scales[:, g + step, :],
+                        rhs=w[:, step, cols.start - first_col : cols.stop - first_col].bitcast(FP8X4),
+                        rhs_scale=planes[offset:P, slot, cols],
+                        start=(g + step == 0),
+                        stop=(g + step == PASSES - 1),
+                    )
+            if i + WEIGHT_BUFS < len(loads):
                 load_weights(i + WEIGHT_BUFS)
-            if g == PASSES - 1:
-                activated[a] = gate_pool.tile([P, HIDDEN], F32, name="activated%d" % a, tag="activated")
-                for j in range(CHUNKS + COMBINE_LAG):
-                    if j < CHUNKS:
-                        activate(a, acc, j)
-                    if j >= COMBINE_LAG:
-                        combine(a, j - COMBINE_LAG)
+            if g + count == PASSES:
+                width = LAST_WIDTH if i == len(loads) - 1 else CHUNK
+                steps = columns // width
+                lag = min(COMBINE_LAG, steps)
+                for s in range(steps + lag):
+                    if s < steps:
+                        start = first_col + s * width
+                        local = start % CHUNK
+                        activate(a, banks[start // CHUNK], slice(local, local + width), slice(start, start + width))
+                    if s >= lag:
+                        start = first_col + (s - lag) * width
+                        combine(a, slice(start, start + width))
                 if a == FORGET:
                     nc.sync.dma_start(out=c_new, in_=c_next[:])

@@ -108,23 +108,23 @@ def tile_forcedgpulstmcell_w_kernel(
                 return a, PACK * (g - X_PASSES)
             return GATES + a // 2, PACK * (X_PASSES * (a % 2) + g)
 
-        def load_scales(a):
+        def load_scales(a, quadrant, queue, dtype):
             x_slot, x_offset = plane_of(a, 0)
             h_slot, h_offset = plane_of(a, X_PASSES)
-            for quadrant in range(QUADRANTS):
-                rows = slice(PACK * quadrant, PACK * (quadrant + 1))
-                first = 32 * quadrant
-                nc.gpsimd.dma_start(
-                    out=planes[first + x_offset : first + x_offset + PACK * X_PASSES, x_slot, :].bitcast(F32),
-                    in_=x_scales[a][:, rows, :].bitcast(F32),
-                )
-                nc.gpsimd.dma_start(
-                    out=planes[first + h_offset : first + h_offset + PACK * H_PASSES, h_slot, :].bitcast(F32),
-                    in_=h_scales[a][:, rows, :].bitcast(F32),
-                )
+            rows = slice(PACK * quadrant, PACK * (quadrant + 1))
+            first = 32 * quadrant
+            queue.dma_start(
+                out=planes[first + x_offset : first + x_offset + PACK * X_PASSES, x_slot, :].bitcast(dtype),
+                in_=x_scales[a][:, rows, :].bitcast(dtype),
+            )
+            queue.dma_start(
+                out=planes[first + h_offset : first + h_offset + PACK * H_PASSES, h_slot, :].bitcast(dtype),
+                in_=h_scales[a][:, rows, :].bitcast(dtype),
+            )
 
         for a in range(GATES):
-            load_scales(a)
+            for quadrant in (2, 3):
+                load_scales(a, quadrant, nc.gpsimd, F32)
 
         loads = [(a, g, 1, 0, HIDDEN) for a in (INPUT, CANDIDATE, FORGET) for g in range(PASSES)]
         for first_col, columns, parts in OUTPUT_GROUPS:
@@ -142,6 +142,11 @@ def tile_forcedgpulstmcell_w_kernel(
 
         for i in range(WEIGHT_BUFS):
             load_weights(i)
+            if i == 1:
+                load_scales(0, 0, nc.sync, I32)
+                load_scales(0, 1, nc.sync, I32)
+            if 2 <= i < 8:
+                load_scales(1 + (i - 2) // 2, (i - 2) % 2, nc.sync, I32)
 
         c_sb = keep.tile([P, HIDDEN], BF16)
         nc.sync.dma_start(out=c_sb[:], in_=c)

@@ -108,23 +108,20 @@ def tile_forcedgpulstmcell_w_kernel(
                 return a, PACK * (g - X_PASSES)
             return GATES + a // 2, PACK * (X_PASSES * (a % 2) + g)
 
-        def load_scales(a, quadrant, queue, dtype):
-            x_slot, x_offset = plane_of(a, 0)
-            h_slot, h_offset = plane_of(a, X_PASSES)
-            rows = slice(PACK * quadrant, PACK * (quadrant + 1))
-            first = 32 * quadrant
+        def load_scales(a, first_pass, count, quadrant, queue, dtype):
+            slot, offset = plane_of(a, first_pass)
+            first = 32 * quadrant + offset
+            source = x_scales[a] if first_pass < X_PASSES else h_scales[a]
             queue.dma_start(
-                out=planes[first + x_offset : first + x_offset + PACK * X_PASSES, x_slot, :].bitcast(dtype),
-                in_=x_scales[a][:, rows, :].bitcast(dtype),
-            )
-            queue.dma_start(
-                out=planes[first + h_offset : first + h_offset + PACK * H_PASSES, h_slot, :].bitcast(dtype),
-                in_=h_scales[a][:, rows, :].bitcast(dtype),
+                out=planes[first : first + PACK * count, slot, :].bitcast(dtype),
+                in_=source[:, PACK * quadrant : PACK * (quadrant + 1), :].bitcast(dtype),
             )
 
         for a in range(GATES):
-            for quadrant in (2, 3):
-                load_scales(a, quadrant, nc.gpsimd, F32)
+            for quadrant in range(QUADRANTS):
+                load_scales(a, 0, X_PASSES, quadrant, nc.gpsimd, F32)
+                if quadrant >= 2:
+                    load_scales(a, X_PASSES, H_PASSES, quadrant, nc.gpsimd, F32)
 
         loads = [(a, g, 1, 0, HIDDEN) for a in (INPUT, CANDIDATE, FORGET) for g in range(PASSES)]
         for first_col, columns, parts in OUTPUT_GROUPS:
@@ -142,11 +139,9 @@ def tile_forcedgpulstmcell_w_kernel(
 
         for i in range(WEIGHT_BUFS):
             load_weights(i)
-            if i == 1:
-                load_scales(0, 0, nc.sync, I32)
-                load_scales(0, 1, nc.sync, I32)
-            if 2 <= i < 8:
-                load_scales(1 + (i - 2) // 2, (i - 2) % 2, nc.sync, I32)
+            if 1 <= i < 8:
+                for n in range(0, 2) if i == 1 else (i,):
+                    load_scales(n // 2, X_PASSES, H_PASSES, n % 2, nc.sync, I32)
 
         c_sb = keep.tile([P, HIDDEN], BF16)
         nc.sync.dma_start(out=c_sb[:], in_=c)

from contextlib import ExitStack

import concourse.mybir as mybir
from concourse.masks import make_identity

F32 = mybir.dt.float32
BF16 = mybir.dt.bfloat16
I32 = mybir.dt.int32
U32 = mybir.dt.uint32
U8 = mybir.dt.uint8
FP8X4 = mybir.dt.float8_e4m3fn_x4
ACT = mybir.ActivationFunctionType

P = 128
PACK = 4
K_PASS = P * PACK
X_PASSES = 2
H_PASSES = 4
PASSES = X_PASSES + H_PASSES
HIDDEN = 2048
CHUNK = 512
CHUNKS = HIDDEN // CHUNK
GATES = 4
QUADRANTS = 4
PLANES_PER_SLOT = 4
PLANE_SLOTS = GATES * PASSES // PLANES_PER_SLOT
WEIGHT_BUFS = 12
COMBINE_LAG = 2
LAST_WIDTH = 256
OUTPUT_GROUPS = (
    (0, 1024, ((0, 2), (2, 2), (4, 2))),
    (1024, 512, ((0, 2), (2, 4))),
    (1536, 512, ((0, 2), (2, 2), (4, 1), (5, 1))),
)

FLOPS = 2 * P * (PASSES * K_PASS) * (GATES * HIDDEN)


def tile_forcedgpulstmcell_w_kernel(
    tc,
    x,
    h,
    c,
    weight_ii_words,
    weight_ii_scales,
    weight_if_words,
    weight_if_scales,
    weight_ig_words,
    weight_ig_scales,
    weight_io_words,
    weight_io_scales,
    weight_hi_words,
    weight_hi_scales,
    weight_hf_words,
    weight_hf_scales,
    weight_hg_words,
    weight_hg_scales,
    weight_ho_words,
    weight_ho_scales,
    bias_i,
    bias_f,
    bias_g,
    bias_o,
    h_new,
    c_new,
):
    nc = tc.nc

    INPUT, CANDIDATE, FORGET, OUTPUT = range(GATES)
    x_words = (weight_ii_words, weight_ig_words, weight_if_words, weight_io_words)
    x_scales = (weight_ii_scales, weight_ig_scales, weight_if_scales, weight_io_scales)
    h_words = (weight_hi_words, weight_hg_words, weight_hf_words, weight_ho_words)
    h_scales = (weight_hi_scales, weight_hg_scales, weight_hf_scales, weight_ho_scales)
    biases = (bias_i, bias_g, bias_f, bias_o)
    functions = (ACT.Sigmoid, ACT.Tanh, ACT.Sigmoid, ACT.Sigmoid)

    with ExitStack() as ctx:
        ctx.enter_context(tc.manual_schedule())
        keep = ctx.enter_context(tc.tile_pool(name="keep", bufs=1))
        weights = ctx.enter_context(tc.tile_pool(name="weights", bufs=WEIGHT_BUFS))
        gate_pool = ctx.enter_context(tc.tile_pool(name="gate", bufs=2))
        work = ctx.enter_context(tc.tile_pool(name="work", bufs=3))
        acc_psum = ctx.enter_context(tc.psum_pool(name="acc", bufs=6))
        aux_psum = ctx.enter_context(tc.psum_pool(name="aux", bufs=2))

        bias_rows = keep.tile([P, CHUNK], BF16)
        nc.vector.memset(bias_rows[:], 0.0)
        planes = keep.tile([P, PLANE_SLOTS, HIDDEN], U8, align_bytes=64)
        nc.vector.memset(planes[:].rearrange("p s n -> p (s n)").bitcast(I32), 0)

        ident_f32 = keep.tile([P, P], F32)
        make_identity(nc, ident_f32[:])
        ident_bf16 = keep.tile([P, P], BF16)
        make_identity(nc, ident_bf16[:])

        z_sb = keep.tile([P, PASSES * K_PASS], BF16)
        nc.sync.dma_start(out=z_sb[:, 0 : X_PASSES * K_PASS], in_=x)
        nc.sync.dma_start(out=z_sb[:, X_PASSES * K_PASS :], in_=h)

        for a in range(GATES):
            nc.scalar.dma_start(
                out=bias_rows[CHUNKS * a : CHUNKS * (a + 1), :],
                in_=biases[a].rearrange("(j n) -> j n", j=CHUNKS),
            )

        def plane_of(a, g):
            if g >= X_PASSES:
                return a, PACK * (g - X_PASSES)
            return GATES + a // 2, PACK * (X_PASSES * (a % 2) + g)

        def load_scales(a, first_pass, count, quadrant, queue, dtype):
            slot, offset = plane_of(a, first_pass)
            first = 32 * quadrant + offset
            source = x_scales[a] if first_pass < X_PASSES else h_scales[a]
            queue.dma_start(
                out=planes[first : first + PACK * count, slot, :].bitcast(dtype),
                in_=source[:, PACK * quadrant : PACK * (quadrant + 1), :].bitcast(dtype),
            )

        for a in range(GATES):
            for quadrant in range(QUADRANTS):
                load_scales(a, 0, X_PASSES, quadrant, nc.gpsimd, F32)
                if quadrant >= 2:
                    load_scales(a, X_PASSES, H_PASSES, quadrant, nc.gpsimd, F32)

        loads = [(a, g, 1, 0, HIDDEN) for a in (INPUT, CANDIDATE, FORGET) for g in range(PASSES)]
        for first_col, columns, parts in OUTPUT_GROUPS:
            for first_pass, count in parts:
                loads.append((OUTPUT, first_pass, count, first_col, columns))
        weight_tiles = {}

        def load_weights(i):
            a, g, count, first_col, columns = loads[i]
            source = x_words[a][g : g + count] if g < X_PASSES else h_words[a][g - X_PASSES : g - X_PASSES + count]
            source = source.rearrange("g p n t -> g p (n t)")[:, :, PACK * first_col : PACK * (first_col + columns)]
            w = weights.tile([P, count, columns], U32, tag="w", align_bytes=64)
            weight_tiles[i] = w
            nc.sync.dma_start(out=w[:].bitcast(I32), in_=source.rearrange("g p b -> p g b").bitcast(I32))

        for i in range(WEIGHT_BUFS):
            load_weights(i)
            if 1 <= i < 8:
                for n in range(0, 2) if i == 1 else (i,):
                    load_scales(n // 2, X_PASSES, H_PASSES, n % 2, nc.sync, I32)

        c_sb = keep.tile([P, HIDDEN], BF16)
        nc.sync.dma_start(out=c_sb[:], in_=c)

        z_words = z_sb[:].bitcast(F32)
        grouped = keep.tile([P, PASSES, P, PACK], BF16, align_bytes=64)
        grouped_words = grouped[:].bitcast(F32)
        for pair in range(PASSES // 2):
            flipped = aux_psum.tile([P, 2, 2, P], F32, tag="aux")
            for half in range(2):
                g = 2 * pair + half
                for u in range(2):
                    nc.tensor.transpose(
                        flipped[:, half, u, :],
                        z_words[:, 256 * g + u : 256 * (g + 1) : 2],
                        ident_f32[:],
                    )
            copy = nc.vector.tensor_copy if pair % 2 == 0 else nc.scalar.copy
            copy(
                out=grouped_words[:, 2 * pair : 2 * pair + 2, :, :],
                in_=flipped[:].rearrange("p g u b -> p g b u"),
            )

        z_codes = keep.tile([P, PASSES, P], U32, align_bytes=64)
        z_scales = keep.tile([P, PASSES, P], U8, align_bytes=64)
        for first, count in ((0, X_PASSES), (X_PASSES, H_PASSES)):
            passes = slice(first, first + count)
            nc.vector.quantize_mx(
                out=z_codes[:, passes, :].rearrange("p g b -> p (g b)").bitcast(FP8X4),
                scales=z_scales[:, passes, :].rearrange("p g b -> p (g b)"),
                in_=grouped[:, passes, :, :].rearrange("p g b t -> p (g b t)"),
            )

        bias_all = keep.tile([P, GATES, HIDDEN], F32)
        for a in range(GATES):
            for j in range(CHUNKS):
                row = CHUNKS * a + j
                spread = aux_psum.tile([P, CHUNK], F32, tag="aux")
                nc.tensor.matmul(
                    spread[:],
                    lhsT=ident_bf16[:, row : row + 1].to_broadcast([P, P]),
                    rhs=bias_rows[:],
                    start=True,
                    stop=True,
                )
                copy = nc.vector.tensor_copy if j % 2 == 0 else nc.scalar.copy
                copy(out=bias_all[:, a, j * CHUNK : (j + 1) * CHUNK], in_=spread[:])

        update = keep.tile([P, HIDDEN], F32)
        c_next = keep.tile([P, HIDDEN], F32)
        tanh_c = keep.tile([P, HIDDEN], F32)
        h_next = keep.tile([P, HIDDEN], F32)
        activated = {}

        def activate(a, bank, local, cols):
            pre = work.tile([P, CHUNK], F32, tag="pre")
            width = cols.stop - cols.start
            nc.vector.tensor_add(out=pre[:, 0:width], in0=bank[:, local], in1=bias_all[:, a, cols])
            nc.scalar.activation(out=activated[a][:, cols], in_=pre[:, 0:width], func=functions[a])

        def combine(a, cols):
            if a == CANDIDATE:
                nc.vector.tensor_mul(out=update[:, cols], in0=activated[INPUT][:, cols], in1=activated[a][:, cols])
            if a == FORGET:
                kept = work.tile([P, CHUNK], F32, tag="kept")
                nc.vector.tensor_mul(out=kept[:], in0=activated[a][:, cols], in1=c_sb[:, cols])
                nc.vector.tensor_add(out=c_next[:, cols], in0=kept[:], in1=update[:, cols])
                nc.scalar.activation(out=tanh_c[:, cols], in_=c_next[:, cols], func=ACT.Tanh)
            if a == OUTPUT:
                nc.vector.tensor_mul(out=h_next[:, cols], in0=activated[a][:, cols], in1=tanh_c[:, cols])
                nc.sync.dma_start(out=h_new[:, cols], in_=h_next[:, cols])

        banks = {}
        for i, (a, g, count, first_col, columns) in enumerate(loads):
            chunks = range(first_col // CHUNK, (first_col + columns) // CHUNK)
            if g == 0:
                if first_col == 0:
                    activated[a] = gate_pool.tile([P, HIDDEN], F32, name="activated%d" % a, tag="activated")
                for j in chunks:
                    banks[j] = acc_psum.tile([P, CHUNK], F32, name="acc%d" % j, tag="acc")
            w = weight_tiles[i]
            for step in range(count):
                slot, offset = plane_of(a, g + step)
                for j in chunks:
                    cols = slice(j * CHUNK, (j + 1) * CHUNK)
                    nc.tensor.matmul_mx(
                        out=banks[j][:],
                        lhsT=z_codes[:, g + step, :].bitcast(FP8X4),
                        lhsT_scale=z_scales[:, g + step, :],
                        rhs=w[:, step, cols.start - first_col : cols.stop - first_col].bitcast(FP8X4),
                        rhs_scale=planes[offset:P, slot, cols],
                        start=(g + step == 0),
                        stop=(g + step == PASSES - 1),
                    )
            if i + WEIGHT_BUFS < len(loads):
                load_weights(i + WEIGHT_BUFS)
            if g + count == PASSES:
                width = LAST_WIDTH if i == len(loads) - 1 else CHUNK
                steps = columns // width
                lag = min(COMBINE_LAG, steps)
                for s in range(steps + lag):
                    if s < steps:
                        start = first_col + s * width
                        local = start % CHUNK
                        activate(a, banks[start // CHUNK], slice(local, local + width), slice(start, start + width))
                    if s >= lag:
                        start = first_col + (s - lag) * width
                        combine(a, slice(start, start + width))
                if a == FORGET:
                    nc.sync.dma_start(out=c_new, in_=c_next[:])
